import numpy as np
import ml_dtypes


def mxq(x, axis, fmt="e4m3"):
    dtype, down = {"e4m3": (ml_dtypes.float8_e4m3fn, 7), "e5m2": (ml_dtypes.float8_e5m2, 14)}[fmt]
    v = np.moveaxis(np.asarray(x, np.float32).astype(ml_dtypes.bfloat16).astype(np.float64), axis, -1)
    blocks = v.reshape(v.shape[:-1] + (-1, 32))
    amax = np.abs(blocks).max(-1, keepdims=True)
    byte = np.maximum(np.where(amax > 0, np.frexp(amax)[1] - 1 + 127, 0) - down, 1)
    scale = np.exp2(byte - 127.0)
    codes = (blocks / scale).astype(np.float32).astype(dtype).astype(np.float64)
    return np.moveaxis((codes * scale).reshape(v.shape), -1, axis)


WIDE = False


def mx_kscale(k):
    if not WIDE:
        return np.ones(k)
    levels = np.array([10, -10, 5, -5, 0])
    if k % 512:
        return np.exp2(np.random.permutation(np.resize(levels, k // 32))).repeat(32)
    a = np.empty((k // 512, 16))
    for p in range(k // 512):
        a[p, :8] = np.random.permutation(np.resize(levels, 8))
        for g in range(8):
            far = levels[np.abs(levels - a[p, g]) >= 10]
            a[p, g + 8] = far[np.random.randint(len(far))]
    return np.exp2(a.ravel()).repeat(32)


BF16 = ml_dtypes.bfloat16


def bf(x):
    return np.asarray(x, np.float32).astype(BF16)


def f64(x):
    return np.asarray(x).astype(np.float64)


B, N, F, O, E, K = 4, 512, 512, 64, 16, 3


def setup_inputs():
    s = mx_kscale(F)
    return {"x_g": bf(np.random.standard_normal((B, K, N, F)) * s),
            "emb": bf(np.random.standard_normal((B, N, E))),
            "weights_pool": bf(np.random.standard_normal((E, K, F, O)) * 0.5 / np.sqrt(K * F) / s[:, None]),
            "bias_pool": bf(np.random.standard_normal((E, O)) * 0.3)}


def reference(x_g, emb, weights_pool, bias_pool):
    xg, w, g = f64(x_g), f64(weights_pool), f64(emb)
    z = 0.0
    for k in range(K):
        wk = w[:, k].transpose(1, 0, 2).reshape(F, E * O)
        z = z + (mxq(xg[:, k], 2, "e4m3") @ mxq(wk, 0, "e4m3"))
    z = z.reshape(B, N, E, O)
    out = (g[:, :, :, None] * z).sum(2)
    return out + (g[:, :, :, None] * f64(bias_pool)[None, None, :, :]).sum(2)

@@ -1,0 +1,192 @@
+from contextlib import ExitStack
+
+import concourse.mybir as mybir
+from concourse.masks import make_identity
+
+BF16 = mybir.dt.bfloat16
+F32 = mybir.dt.float32
+U32 = mybir.dt.uint32
+U8 = mybir.dt.uint8
+FP8X4 = mybir.dt.float8_e4m3fn_x4
+MULT = mybir.AluOpType.mult
+ADD = mybir.AluOpType.add
+
+P = 128
+PACK = 4
+BATCH, ORDERS, NODES, FEAT = 4, 3, 512, 512
+SETS, OUT = 16, 64
+TILES = NODES // P
+ROWS = BATCH * TILES
+HALVES = 2
+WORDS = FEAT // 2
+BANK = 512
+ROUND_SETS = 4
+ROUNDS = SETS // ROUND_SETS
+ROUND_COLS = ROUND_SETS * OUT
+BANK_TILES = BANK // ROUND_COLS
+SLOTS = 2
+
+FLOPS = 2 * BATCH * NODES * ORDERS * FEAT * SETS * OUT
+
+
+def tile_dygcn_pb_kernel(tc, x_g, emb, weights_pool, bias_pool, out):
+    nc = tc.nc
+    with ExitStack() as ctx:
+        keep = ctx.enter_context(tc.tile_pool(name="keep", bufs=1))
+        stage = ctx.enter_context(tc.tile_pool(name="stage", bufs=3))
+        psum_x = ctx.enter_context(tc.psum_pool(name="psum_x", bufs=4))
+        psum_z = ctx.enter_context(tc.psum_pool(name="psum_z", bufs=4))
+
+        x_raw = [keep.tile([P, ORDERS * TILES * FEAT], BF16, name="x_raw%d" % b) for b in range(BATCH)]
+        w_raw = [keep.tile([P, ORDERS, ROUND_SETS, PACK * OUT], BF16, name="w_raw%d" % r) for r in range(ROUNDS)]
+        x_codes = keep.tile([P, BATCH * ORDERS, TILES * P], U32, align_bytes=64)
+        x_scales = keep.tile([P, BATCH * ORDERS, TILES * P], U8, align_bytes=64)
+        w_codes = keep.tile([P, ROUNDS * ORDERS, ROUND_COLS], U32, align_bytes=64)
+        w_scales = keep.tile([P, ROUNDS * ORDERS, ROUND_COLS], U8, align_bytes=64)
+        acc = keep.tile([P, SLOTS, ROWS, OUT], F32)
+
+        def load_x(b):
+            for k in range(ORDERS):
+                nc.sync.dma_start(
+                    out=x_raw[b][:, k * TILES * FEAT : (k + 1) * TILES * FEAT],
+                    in_=x_g[b, k].rearrange("(p t) f -> p (t f)", t=TILES),
+                )
+
+        def load_w(r):
+            for k in range(ORDERS):
+                nc.sync.dma_start(
+                    out=w_raw[r][:, k, :, :],
+                    in_=weights_pool[r * ROUND_SETS : (r + 1) * ROUND_SETS, k, :, :].rearrange(
+                        "e (p j) o -> p e (j o)", j=PACK
+                    ),
+                )
+
+        load_x(0)
+        load_w(0)
+        for b in range(1, BATCH):
+            load_x(b)
+        for r in range(1, ROUNDS):
+            load_w(r)
+
+        ident = keep.tile([P, P], F32)
+        make_identity(nc, ident[:])
+        emb_bf = keep.tile([P, BATCH, TILES * SETS], BF16)
+        nc.scalar.dma_start(out=emb_bf[:], in_=emb.rearrange("b (p t) e -> p b (t e)", t=TILES))
+        DIAG = P // SETS
+        GROUPS = ROWS // DIAG
+        bias_diag = keep.tile([P, DIAG * OUT], BF16)
+        nc.vector.memset(bias_diag[:], 0.0)
+        for d in range(DIAG):
+            nc.scalar.dma_start(
+                out=bias_diag[d * SETS : (d + 1) * SETS, d * OUT : (d + 1) * OUT], in_=bias_pool
+            )
+        nc.vector.memset(acc[:, 1, :, :], 0.0)
+        emb_f32 = keep.tile([P, ROWS * SETS], F32)
+        nc.vector.tensor_copy(out=emb_f32[:], in_=emb_bf[:].rearrange("p b c -> p (b c)"))
+        emb_t_ps = psum_x.tile([P, GROUPS, P], F32, name="xt")
+        for g in range(GROUPS):
+            nc.tensor.transpose(emb_t_ps[:, g, :], emb_f32[:, g * P : (g + 1) * P], ident[:])
+        emb_t = keep.tile([P, GROUPS, P], BF16)
+        nc.vector.tensor_copy(out=emb_t[:], in_=emb_t_ps[:])
+
+        def bias_term():
+            for g in range(GROUPS):
+                bias_ps = psum_z.tile([P, DIAG * OUT], F32, name="z")
+                nc.tensor.matmul(bias_ps[:], lhsT=emb_t[:, g, :], rhs=bias_diag[:], start=True, stop=True)
+                nc.scalar.copy(
+                    out=acc[:, 0, g * DIAG : (g + 1) * DIAG, :].rearrange("p d o -> p (d o)"), in_=bias_ps[:]
+                )
+
+        def prepare_w(r):
+            for k in range(ORDERS):
+                grouped = stage.tile([P, ROUND_COLS, PACK], BF16, align_bytes=64, name="w_grouped")
+                if k == 0:
+                    nc.scalar.copy(
+                        out=grouped[:].rearrange("p (e o) j -> p e o j", o=OUT),
+                        in_=w_raw[r][:, k, :, :].rearrange("p e (j o) -> p e o j", j=PACK),
+                    )
+                else:
+                    nc.vector.tensor_copy(
+                        out=grouped[:].rearrange("p (e c i) j -> p e c j i", e=ROUND_SETS, i=4),
+                        in_=w_raw[r][:, k, :, :].rearrange("p e (j c i) -> p e c j i", j=PACK, i=4),
+                    )
+                nc.vector.quantize_mx(
+                    out=w_codes[:, r * ORDERS + k, :].bitcast(FP8X4),
+                    scales=w_scales[:, r * ORDERS + k, :],
+                    in_=grouped[:].rearrange("p c j -> p (c j)"),
+                )
+
+        def prepare_x(b):
+            x_words = x_raw[b][:].bitcast(F32)
+            for k in range(ORDERS):
+                grouped = stage.tile([P, TILES * P * PACK], BF16, align_bytes=64, name="x_grouped")
+                grouped_words = grouped[:].bitcast(F32).rearrange("p (t n u) -> p t n u", t=TILES, u=HALVES)
+                for pair in range(TILES // 2):
+                    xt = psum_x.tile([P, 2, HALVES, P], F32, name="xt")
+                    for i in range(2):
+                        row = (k * TILES + 2 * pair + i) * WORDS
+                        for u in range(HALVES):
+                            nc.tensor.transpose(
+                                xt[:, i, u, :], x_words[:, row + u : row + WORDS : HALVES], ident[:]
+                            )
+                    nc.scalar.copy(
+                        out=grouped_words[:, 2 * pair : 2 * pair + 2, :, :],
+                        in_=xt[:].rearrange("p i u n -> p i n u"),
+                    )
+                nc.vector.quantize_mx(
+                    out=x_codes[:, b * ORDERS + k, :].bitcast(FP8X4),
+                    scales=x_scales[:, b * ORDERS + k, :],
+                    in_=grouped[:],
+                )
+
+        def batch_round(r, b):
+            banks = []
+            for j in range(TILES // BANK_TILES):
+                z = psum_z.tile([P, BANK_TILES, ROUND_COLS], F32, name="z")
+                banks.append(z)
+                for i in range(BANK_TILES):
+                    t = j * BANK_TILES + i
+                    for k in range(ORDERS):
+                        nc.tensor.matmul_mx(
+                            out=z[:, i, :],
+                            lhsT=x_codes[:, b * ORDERS + k, t * P : (t + 1) * P].bitcast(FP8X4),
+                            lhsT_scale=x_scales[:, b * ORDERS + k, t * P : (t + 1) * P],
+                            rhs=w_codes[:, r * ORDERS + k, :].bitcast(FP8X4),
+                            rhs_scale=w_scales[:, r * ORDERS + k, :],
+                            start=(k == 0),
+                            stop=(k == ORDERS - 1),
+                        )
+            for s in range(ROUND_SETS):
+                for t in range(TILES):
+                    row = b * TILES + t
+                    col = row * SETS + r * ROUND_SETS + s
+                    nc.vector.scalar_tensor_tensor(
+                        out=acc[:, s % SLOTS, row, :],
+                        in0=banks[t // BANK_TILES][:, t % BANK_TILES, s * OUT : (s + 1) * OUT],
+                        scalar=emb_f32[:, col : col + 1],
+                        in1=acc[:, s % SLOTS, row, :],
+                        op0=MULT,
+                        op1=ADD,
+                    )
+
+        def store(b):
+            rows = slice(b * TILES, (b + 1) * TILES)
+            result = stage.tile([P, TILES, OUT], F32, name="result")
+            nc.vector.tensor_add(out=result[:], in0=acc[:, 0, rows, :], in1=acc[:, 1, rows, :])
+            nc.sync.dma_start(
+                out=out[b].rearrange("(p t) o -> p (t o)", t=TILES),
+                in_=result[:].rearrange("p t o -> p (t o)"),
+            )
+
+        prepare_x(0)
+        prepare_w(0)
+        bias_term()
+        for r in range(ROUNDS):
+            for b in range(BATCH):
+                if r == 0 and b + 1 < BATCH:
+                    prepare_x(b + 1)
+                if r + 1 < ROUNDS and b == BATCH - 1:
+                    prepare_w(r + 1)
+                batch_round(r, b)
+                if r == ROUNDS - 1:
+                    store(b)

@@ -17,13 +17,12 @@ BATCH, ORDERS, NODES, FEAT = 4, 3, 512, 512
 SETS, OUT = 16, 64
 TILES = NODES // P
 ROWS = BATCH * TILES
-HALVES = 2
+PAIR = 2
+HALVES = ROWS // PAIR
 WORDS = FEAT // 2
-BANK = 512
 ROUND_SETS = 4
 ROUNDS = SETS // ROUND_SETS
 ROUND_COLS = ROUND_SETS * OUT
-BANK_TILES = BANK // ROUND_COLS
 SLOTS = 2
 
 FLOPS = 2 * BATCH * NODES * ORDERS * FEAT * SETS * OUT
@@ -33,160 +32,223 @@ def tile_dygcn_pb_kernel(tc, x_g, emb, weights_pool, bias_pool, out):
     nc = tc.nc
     with ExitStack() as ctx:
         keep = ctx.enter_context(tc.tile_pool(name="keep", bufs=1))
-        stage = ctx.enter_context(tc.tile_pool(name="stage", bufs=3))
-        psum_x = ctx.enter_context(tc.psum_pool(name="psum_x", bufs=4))
-        psum_z = ctx.enter_context(tc.psum_pool(name="psum_z", bufs=4))
+        stage = ctx.enter_context(tc.tile_pool(name="stage", bufs=6))
+        psum = ctx.enter_context(tc.psum_pool(name="psum", bufs=8))
+        ctx.enter_context(tc.manual_schedule())
 
-        x_raw = [keep.tile([P, ORDERS * TILES * FEAT], BF16, name="x_raw%d" % b) for b in range(BATCH)]
-        w_raw = [keep.tile([P, ORDERS, ROUND_SETS, PACK * OUT], BF16, name="w_raw%d" % r) for r in range(ROUNDS)]
-        x_codes = keep.tile([P, BATCH * ORDERS, TILES * P], U32, align_bytes=64)
-        x_scales = keep.tile([P, BATCH * ORDERS, TILES * P], U8, align_bytes=64)
-        w_codes = keep.tile([P, ROUNDS * ORDERS, ROUND_COLS], U32, align_bytes=64)
-        w_scales = keep.tile([P, ROUNDS * ORDERS, ROUND_COLS], U8, align_bytes=64)
+        x_raw = [
+            [keep.tile([P, PAIR * FEAT], BF16, name="x_raw%d_%d" % (h, k)) for k in range(ORDERS)]
+            for h in range(HALVES)
+        ]
+        w_raw = [
+            [keep.tile([P, ROUND_SETS, PACK * OUT], BF16, name="w_raw%d_%d" % (r, k)) for k in range(ORDERS)]
+            for r in range(ROUNDS)
+        ]
+        x_codes = [keep.tile([P, ORDERS, PAIR * P], U32, align_bytes=64, name="x_codes%d" % h) for h in range(HALVES)]
+        x_scales = [keep.tile([P, ORDERS, PAIR * P], U8, align_bytes=64, name="x_scales%d" % h) for h in range(HALVES)]
+        w_codes = [keep.tile([P, ORDERS, ROUND_COLS], U32, align_bytes=64, name="w_codes%d" % r) for r in range(ROUNDS)]
+        w_scales = [keep.tile([P, ORDERS, ROUND_COLS], U8, align_bytes=64, name="w_scales%d" % r) for r in range(ROUNDS)]
         acc = keep.tile([P, SLOTS, ROWS, OUT], F32)
 
-        def load_x(b):
+        warm_in = keep.tile([P, 1], F32)
+        warm_out = keep.tile([P, 1], F32)
+        nc.vector.memset(warm_in[:], 0.0)
+        nc.scalar.copy(out=warm_out[:], in_=warm_in[:])
+
+        ident = keep.tile([P, P], F32)
+        make_identity(nc, ident[:])
+
+        def load_x(h):
+            b, pr = divmod(h, TILES // PAIR)
             for k in range(ORDERS):
                 nc.sync.dma_start(
-                    out=x_raw[b][:, k * TILES * FEAT : (k + 1) * TILES * FEAT],
-                    in_=x_g[b, k].rearrange("(p t) f -> p (t f)", t=TILES),
+                    out=x_raw[h][k][:],
+                    in_=x_g[b, k].rearrange("(p t) f -> p (t f)", t=TILES)[
+                        :, pr * PAIR * FEAT : (pr + 1) * PAIR * FEAT
+                    ],
                 )
 
         def load_w(r):
             for k in range(ORDERS):
                 nc.sync.dma_start(
-                    out=w_raw[r][:, k, :, :],
+                    out=w_raw[r][k][:],
                     in_=weights_pool[r * ROUND_SETS : (r + 1) * ROUND_SETS, k, :, :].rearrange(
                         "e (p j) o -> p e (j o)", j=PACK
                     ),
                 )
 
-        load_x(0)
-        load_w(0)
-        for b in range(1, BATCH):
-            load_x(b)
-        for r in range(1, ROUNDS):
-            load_w(r)
-
-        ident = keep.tile([P, P], F32)
-        make_identity(nc, ident[:])
         emb_bf = keep.tile([P, BATCH, TILES * SETS], BF16)
         nc.scalar.dma_start(out=emb_bf[:], in_=emb.rearrange("b (p t) e -> p b (t e)", t=TILES))
         DIAG = P // SETS
         GROUPS = ROWS // DIAG
         bias_diag = keep.tile([P, DIAG * OUT], BF16)
-        nc.vector.memset(bias_diag[:], 0.0)
+        nc.gpsimd.memset(bias_diag[:], 0.0)
         for d in range(DIAG):
-            nc.scalar.dma_start(
+            nc.gpsimd.dma_start(
                 out=bias_diag[d * SETS : (d + 1) * SETS, d * OUT : (d + 1) * OUT], in_=bias_pool
             )
-        nc.vector.memset(acc[:, 1, :, :], 0.0)
-        emb_f32 = keep.tile([P, ROWS * SETS], F32)
-        nc.vector.tensor_copy(out=emb_f32[:], in_=emb_bf[:].rearrange("p b c -> p (b c)"))
-        emb_t_ps = psum_x.tile([P, GROUPS, P], F32, name="xt")
-        for g in range(GROUPS):
-            nc.tensor.transpose(emb_t_ps[:, g, :], emb_f32[:, g * P : (g + 1) * P], ident[:])
-        emb_t = keep.tile([P, GROUPS, P], BF16)
-        nc.vector.tensor_copy(out=emb_t[:], in_=emb_t_ps[:])
 
-        def bias_term():
-            for g in range(GROUPS):
-                bias_ps = psum_z.tile([P, DIAG * OUT], F32, name="z")
-                nc.tensor.matmul(bias_ps[:], lhsT=emb_t[:, g, :], rhs=bias_diag[:], start=True, stop=True)
-                nc.scalar.copy(
-                    out=acc[:, 0, g * DIAG : (g + 1) * DIAG, :].rearrange("p d o -> p (d o)"), in_=bias_ps[:]
+        load_x(0)
+        load_w(0)
+        for h in range(1, 5):
+            load_x(h)
+        load_w(1)
+        for h in range(5, HALVES):
+            load_x(h)
+        load_w(2)
+        load_w(3)
+
+
+        w_grouped = [
+            [keep.tile([P, ROUND_COLS, PACK], BF16, align_bytes=64, name="w_grouped%d_%d" % (r, k)) for k in range(ORDERS)]
+            for r in range(ROUNDS)
+        ]
+
+        def regroup_w(r, k, on_vector):
+            if on_vector:
+                nc.vector.tensor_copy(
+                    out=w_grouped[r][k][:].rearrange("p (e c i) j -> p e c j i", e=ROUND_SETS, i=4),
+                    in_=w_raw[r][k][:].rearrange("p e (j c i) -> p e c j i", j=PACK, i=4),
+                )
+            else:
+                nc.gpsimd.tensor_scalar(
+                    out=w_grouped[r][k][:].rearrange("p (e o) j -> p e o j", o=OUT),
+                    in0=w_raw[r][k][:].rearrange("p e (j o) -> p e o j", j=PACK),
+                    scalar1=1.0,
+                    scalar2=0.0,
+                    op0=MULT,
+                    op1=ADD,
                 )
 
-        def prepare_w(r):
+        def quantise_w(r, k):
+            nc.vector.quantize_mx(
+                out=w_codes[r][:, k, :].bitcast(FP8X4),
+                scales=w_scales[r][:, k, :],
+                in_=w_grouped[r][k][:].rearrange("p c j -> p (c j)"),
+            )
+
+        for r in range(1, ROUNDS):
             for k in range(ORDERS):
-                grouped = stage.tile([P, ROUND_COLS, PACK], BF16, align_bytes=64, name="w_grouped")
-                if k == 0:
-                    nc.scalar.copy(
-                        out=grouped[:].rearrange("p (e o) j -> p e o j", o=OUT),
-                        in_=w_raw[r][:, k, :, :].rearrange("p e (j o) -> p e o j", j=PACK),
-                    )
-                else:
-                    nc.vector.tensor_copy(
-                        out=grouped[:].rearrange("p (e c i) j -> p e c j i", e=ROUND_SETS, i=4),
-                        in_=w_raw[r][:, k, :, :].rearrange("p e (j c i) -> p e c j i", j=PACK, i=4),
-                    )
-                nc.vector.quantize_mx(
-                    out=w_codes[:, r * ORDERS + k, :].bitcast(FP8X4),
-                    scales=w_scales[:, r * ORDERS + k, :],
-                    in_=grouped[:].rearrange("p c j -> p (c j)"),
-                )
+                regroup_w(r, k, False)
 
-        def prepare_x(b):
-            x_words = x_raw[b][:].bitcast(F32)
+        x_grouped = {}
+
+        def transpose_x(h):
             for k in range(ORDERS):
-                grouped = stage.tile([P, TILES * P * PACK], BF16, align_bytes=64, name="x_grouped")
-                grouped_words = grouped[:].bitcast(F32).rearrange("p (t n u) -> p t n u", t=TILES, u=HALVES)
-                for pair in range(TILES // 2):
-                    xt = psum_x.tile([P, 2, HALVES, P], F32, name="xt")
-                    for i in range(2):
-                        row = (k * TILES + 2 * pair + i) * WORDS
-                        for u in range(HALVES):
-                            nc.tensor.transpose(
-                                xt[:, i, u, :], x_words[:, row + u : row + WORDS : HALVES], ident[:]
-                            )
-                    nc.scalar.copy(
-                        out=grouped_words[:, 2 * pair : 2 * pair + 2, :, :],
-                        in_=xt[:].rearrange("p i u n -> p i n u"),
-                    )
-                nc.vector.quantize_mx(
-                    out=x_codes[:, b * ORDERS + k, :].bitcast(FP8X4),
-                    scales=x_scales[:, b * ORDERS + k, :],
-                    in_=grouped[:],
-                )
-
-        def batch_round(r, b):
-            banks = []
-            for j in range(TILES // BANK_TILES):
-                z = psum_z.tile([P, BANK_TILES, ROUND_COLS], F32, name="z")
-                banks.append(z)
-                for i in range(BANK_TILES):
-                    t = j * BANK_TILES + i
-                    for k in range(ORDERS):
-                        nc.tensor.matmul_mx(
-                            out=z[:, i, :],
-                            lhsT=x_codes[:, b * ORDERS + k, t * P : (t + 1) * P].bitcast(FP8X4),
-                            lhsT_scale=x_scales[:, b * ORDERS + k, t * P : (t + 1) * P],
-                            rhs=w_codes[:, r * ORDERS + k, :].bitcast(FP8X4),
-                            rhs_scale=w_scales[:, r * ORDERS + k, :],
-                            start=(k == 0),
-                            stop=(k == ORDERS - 1),
+                words = x_raw[h][k][:].bitcast(F32)
+                xt = psum.tile([P, PAIR, 2, P], F32, name="bank")
+                for i in range(PAIR):
+                    for u in range(2):
+                        nc.tensor.transpose(
+                            xt[:, i, u, :], words[:, i * WORDS + u : (i + 1) * WORDS : 2], ident[:]
                         )
-            for s in range(ROUND_SETS):
-                for t in range(TILES):
-                    row = b * TILES + t
-                    col = row * SETS + r * ROUND_SETS + s
-                    nc.vector.scalar_tensor_tensor(
-                        out=acc[:, s % SLOTS, row, :],
-                        in0=banks[t // BANK_TILES][:, t % BANK_TILES, s * OUT : (s + 1) * OUT],
-                        scalar=emb_f32[:, col : col + 1],
-                        in1=acc[:, s % SLOTS, row, :],
-                        op0=MULT,
-                        op1=ADD,
-                    )
+                grouped = stage.tile([P, PAIR * P * PACK], BF16, align_bytes=64, name="x_grouped")
+                x_grouped[(h, k)] = grouped
+                nc.scalar.copy(
+                    out=grouped[:].bitcast(F32).rearrange("p (i n u) -> p i n u", i=PAIR, u=2),
+                    in_=xt[:].rearrange("p i u n -> p i n u"),
+                )
 
-        def store(b):
-            rows = slice(b * TILES, (b + 1) * TILES)
-            result = stage.tile([P, TILES, OUT], F32, name="result")
+        def quantise_x(h, k):
+            nc.vector.quantize_mx(
+                out=x_codes[h][:, k, :].bitcast(FP8X4),
+                scales=x_scales[h][:, k, :],
+                in_=x_grouped[(h, k)][:],
+            )
+
+        def half_round(h, r):
+            z = psum.tile([P, PAIR, ROUND_COLS], F32, name="bank")
+            for i in range(PAIR):
+                for k in range(ORDERS):
+                    nc.tensor.matmul_mx(
+                        out=z[:, i, :],
+                        lhsT=x_codes[h][:, k, i * P : (i + 1) * P].bitcast(FP8X4),
+                        lhsT_scale=x_scales[h][:, k, i * P : (i + 1) * P],
+                        rhs=w_codes[r][:, k, :].bitcast(FP8X4),
+                        rhs_scale=w_scales[r][:, k, :],
+                        start=(k == 0),
+                        stop=(k == ORDERS - 1),
+                    )
+            for s in range(ROUND_SETS):
+                for i in range(PAIR):
+                    row = h * PAIR + i
+                    col = row * SETS + r * ROUND_SETS + s
+                    if r == 0 and s < SLOTS:
+                        nc.vector.tensor_scalar(
+                            out=acc[:, s, row, :],
+                            in0=z[:, i, s * OUT : (s + 1) * OUT],
+                            scalar1=emb_f32[:, col : col + 1],
+                            scalar2=None,
+                            op0=MULT,
+                        )
+                    else:
+                        nc.vector.scalar_tensor_tensor(
+                            out=acc[:, s % SLOTS, row, :],
+                            in0=z[:, i, s * OUT : (s + 1) * OUT],
+                            scalar=emb_f32[:, col : col + 1],
+                            in1=acc[:, s % SLOTS, row, :],
+                            op0=MULT,
+                            op1=ADD,
+                        )
+
+        def store(h):
+            b, pr = divmod(h, TILES // PAIR)
+            rows = slice(h * PAIR, (h + 1) * PAIR)
+            result = stage.tile([P, PAIR, OUT], F32, name="result")
             nc.vector.tensor_add(out=result[:], in0=acc[:, 0, rows, :], in1=acc[:, 1, rows, :])
             nc.sync.dma_start(
-                out=out[b].rearrange("(p t) o -> p (t o)", t=TILES),
+                out=out[b].rearrange("(p t) o -> p (t o)", t=TILES)[:, pr * PAIR * OUT : (pr + 1) * PAIR * OUT],
                 in_=result[:].rearrange("p t o -> p (t o)"),
             )
 
-        prepare_x(0)
-        prepare_w(0)
-        bias_term()
-        for r in range(ROUNDS):
-            for b in range(BATCH):
-                if r == 0 and b + 1 < BATCH:
-                    prepare_x(b + 1)
-                if r + 1 < ROUNDS and b == BATCH - 1:
-                    prepare_w(r + 1)
-                batch_round(r, b)
+        emb_f32 = keep.tile([P, ROWS * SETS], F32)
+        emb_t = keep.tile([P, GROUPS, P], BF16)
+
+        def emb_transposed():
+            emb_t_ps = psum.tile([P, GROUPS, P], F32, name="bank")
+            for g in range(GROUPS):
+                nc.tensor.transpose(emb_t_ps[:, g, :], emb_f32[:, g * P : (g + 1) * P], ident[:])
+            nc.scalar.copy(out=emb_t[:], in_=emb_t_ps[:])
+
+        def bias_term(g):
+            bias_ps = psum.tile([P, DIAG * OUT], F32, name="bank")
+            nc.tensor.matmul(bias_ps[:], lhsT=emb_t[:, g, :], rhs=bias_diag[:], start=True, stop=True)
+            rows = acc[:, 0, g * DIAG : (g + 1) * DIAG, :].rearrange("p d o -> p (d o)")
+            nc.vector.tensor_add(out=rows, in0=bias_ps[:], in1=rows)
+
+        nc.vector.tensor_copy(out=emb_f32[:], in_=emb_bf[:].rearrange("p b c -> p (b c)"))
+        transpose_x(0)
+        quantise_x(0, 0)
+        regroup_w(0, 0, True)
+        quantise_x(0, 1)
+        regroup_w(0, 1, True)
+        quantise_w(0, 0)
+        quantise_x(0, 2)
+        regroup_w(0, 2, True)
+        quantise_w(0, 1)
+        transpose_x(1)
+        quantise_x(1, 0)
+        quantise_w(0, 2)
+        quantise_x(1, 1)
+        quantise_x(1, 2)
+
+        for h in range(HALVES):
+            half_round(h, 0)
+            if h + 2 < HALVES:
+                transpose_x(h + 2)
+                for k in range(ORDERS):
+                    quantise_x(h + 2, k)
+            if h == 3:
+                emb_transposed()
+            if h == 5:
+                for k in range(ORDERS):
+                    quantise_w(1, k)
+                bias_term(0)
+        bias_term(1)
+        for r in range(1, ROUNDS):
+            for h in range(HALVES):
+                half_round(h, r)
+                if r + 1 < ROUNDS and 1 <= h <= ORDERS:
+                    quantise_w(r + 1, h - 1)
                 if r == ROUNDS - 1:
-                    store(b)
+                    store(h)

@@ -82,19 +82,23 @@ def tile_dygcn_pb_kernel(tc, x_g, emb, weights_pool, bias_pool, out):
         DIAG = P // SETS
         GROUPS = ROWS // DIAG
         bias_diag = keep.tile([P, DIAG * OUT], BF16)
-        nc.gpsimd.memset(bias_diag[:], 0.0)
-        for d in range(DIAG):
-            nc.gpsimd.dma_start(
+        nc.vector.memset(bias_diag[:], 0.0)
+
+        def load_bias(d):
+            nc.sync.dma_start(
                 out=bias_diag[d * SETS : (d + 1) * SETS, d * OUT : (d + 1) * OUT], in_=bias_pool
             )
 
         load_x(0)
         load_w(0)
+        load_bias(0)
         for h in range(1, 5):
             load_x(h)
+            load_bias(h)
         load_w(1)
         for h in range(5, HALVES):
             load_x(h)
+            load_bias(h)
         load_w(2)
         load_w(3)
 
@@ -111,13 +115,9 @@ def tile_dygcn_pb_kernel(tc, x_g, emb, weights_pool, bias_pool, out):
                     in_=w_raw[r][k][:].rearrange("p e (j c i) -> p e c j i", j=PACK, i=4),
                 )
             else:
-                nc.gpsimd.tensor_scalar(
+                nc.scalar.copy(
                     out=w_grouped[r][k][:].rearrange("p (e o) j -> p e o j", o=OUT),
-                    in0=w_raw[r][k][:].rearrange("p e (j o) -> p e o j", j=PACK),
-                    scalar1=1.0,
-                    scalar2=0.0,
-                    op0=MULT,
-                    op1=ADD,
+                    in_=w_raw[r][k][:].rearrange("p e (j o) -> p e o j", j=PACK),
                 )
 
         def quantise_w(r, k):
@@ -126,10 +126,6 @@ def tile_dygcn_pb_kernel(tc, x_g, emb, weights_pool, bias_pool, out):
                 scales=w_scales[r][:, k, :],
                 in_=w_grouped[r][k][:].rearrange("p c j -> p (c j)"),
             )
-
-        for r in range(1, ROUNDS):
-            for k in range(ORDERS):
-                regroup_w(r, k, False)
 
         x_grouped = {}
 
@@ -156,8 +152,11 @@ def tile_dygcn_pb_kernel(tc, x_g, emb, weights_pool, bias_pool, out):
                 in_=x_grouped[(h, k)][:],
             )
 
-        def half_round(h, r):
+        banks = {}
+
+        def passes(h, r):
             z = psum.tile([P, PAIR, ROUND_COLS], F32, name="bank")
+            banks[(h, r)] = z
             for i in range(PAIR):
                 for k in range(ORDERS):
                     nc.tensor.matmul_mx(
@@ -169,11 +168,14 @@ def tile_dygcn_pb_kernel(tc, x_g, emb, weights_pool, bias_pool, out):
                         start=(k == 0),
                         stop=(k == ORDERS - 1),
                     )
-            for s in range(ROUND_SETS):
+
+        def sums(h, r, part):
+            z = banks[(h, r)]
+            for s in range(part * SLOTS, (part + 1) * SLOTS):
                 for i in range(PAIR):
                     row = h * PAIR + i
                     col = row * SETS + r * ROUND_SETS + s
-                    if r == 0 and s < SLOTS:
+                    if r == 0 and part == 0:
                         nc.vector.tensor_scalar(
                             out=acc[:, s, row, :],
                             in0=z[:, i, s * OUT : (s + 1) * OUT],
@@ -233,22 +235,40 @@ def tile_dygcn_pb_kernel(tc, x_g, emb, weights_pool, bias_pool, out):
         quantise_x(1, 2)
 
         for h in range(HALVES):
-            half_round(h, 0)
+            passes(h, 0)
+            sums(h, 0, 0)
+            if h > 0:
+                sums(h - 1, 0, 1)
             if h + 2 < HALVES:
                 transpose_x(h + 2)
                 for k in range(ORDERS):
                     quantise_x(h + 2, k)
             if h == 3:
                 emb_transposed()
+                regroup_w(1, 0, False)
+            if h == 4:
+                regroup_w(1, 1, False)
+                regroup_w(1, 2, True)
+                quantise_w(1, 0)
             if h == 5:
-                for k in range(ORDERS):
-                    quantise_w(1, k)
+                quantise_w(1, 1)
+                quantise_w(1, 2)
                 bias_term(0)
         bias_term(1)
+        for r in range(2, ROUNDS):
+            for k in range(ORDERS):
+                regroup_w(r, k, False)
         for r in range(1, ROUNDS):
             for h in range(HALVES):
-                half_round(h, r)
-                if r + 1 < ROUNDS and 1 <= h <= ORDERS:
-                    quantise_w(r + 1, h - 1)
-                if r == ROUNDS - 1:
-                    store(h)
+                passes(h, r)
+                sums(h, r, 0)
+                if h > 0:
+                    sums(h - 1, r, 1)
+                    if r == ROUNDS - 1:
+                        store(h - 1)
+                else:
+                    sums(HALVES - 1, r - 1, 1)
+                if r + 1 < ROUNDS and 4 <= h < 4 + ORDERS:
+                    quantise_w(r + 1, h - 4)
+        sums(HALVES - 1, ROUNDS - 1, 1)
+        store(HALVES - 1)

@@ -34,7 +34,7 @@ def tile_dygcn_pb_kernel(tc, x_g, emb, weights_pool, bias_pool, out):
         keep = ctx.enter_context(tc.tile_pool(name="keep", bufs=1))
         stage = ctx.enter_context(tc.tile_pool(name="stage", bufs=6))
         psum = ctx.enter_context(tc.psum_pool(name="psum", bufs=8))
-        ctx.enter_context(tc.manual_schedule())
+        ctx.enter_context(tc.manual_schedule(engines={mybir.EngineType.PE}))
 
         x_raw = [
             [keep.tile([P, PAIR * FEAT], BF16, name="x_raw%d_%d" % (h, k)) for k in range(ORDERS)]
@@ -233,16 +233,19 @@ def tile_dygcn_pb_kernel(tc, x_g, emb, weights_pool, bias_pool, out):
         quantise_w(0, 2)
         quantise_x(1, 1)
         quantise_x(1, 2)
+        transpose_x(2)
+        for k in range(ORDERS):
+            quantise_x(2, k)
 
         for h in range(HALVES):
             passes(h, 0)
             sums(h, 0, 0)
             if h > 0:
                 sums(h - 1, 0, 1)
-            if h + 2 < HALVES:
-                transpose_x(h + 2)
+            if h + 3 < HALVES:
+                transpose_x(h + 3)
                 for k in range(ORDERS):
-                    quantise_x(h + 2, k)
+                    quantise_x(h + 3, k)
             if h == 3:
                 emb_transposed()
                 regroup_w(1, 0, False)

@@ -24,6 +24,7 @@ ROUND_SETS = 4
 ROUNDS = SETS // ROUND_SETS
 ROUND_COLS = ROUND_SETS * OUT
 SLOTS = 2
+LAG = 3
 
 FLOPS = 2 * BATCH * NODES * ORDERS * FEAT * SETS * OUT
 
@@ -34,7 +35,7 @@ def tile_dygcn_pb_kernel(tc, x_g, emb, weights_pool, bias_pool, out):
         keep = ctx.enter_context(tc.tile_pool(name="keep", bufs=1))
         stage = ctx.enter_context(tc.tile_pool(name="stage", bufs=6))
         psum = ctx.enter_context(tc.psum_pool(name="psum", bufs=8))
-        ctx.enter_context(tc.manual_schedule(engines={mybir.EngineType.PE}))
+        ctx.enter_context(tc.manual_schedule(engines={mybir.EngineType.PE, mybir.EngineType.Activation}))
 
         x_raw = [
             [keep.tile([P, PAIR * FEAT], BF16, name="x_raw%d_%d" % (h, k)) for k in range(ORDERS)]
@@ -92,11 +93,11 @@ def tile_dygcn_pb_kernel(tc, x_g, emb, weights_pool, bias_pool, out):
         load_x(0)
         load_w(0)
         load_bias(0)
-        for h in range(1, 5):
+        for h in range(1, 3):
             load_x(h)
             load_bias(h)
         load_w(1)
-        for h in range(5, HALVES):
+        for h in range(3, HALVES):
             load_x(h)
             load_bias(h)
         load_w(2)
@@ -233,45 +234,49 @@ def tile_dygcn_pb_kernel(tc, x_g, emb, weights_pool, bias_pool, out):
         quantise_w(0, 2)
         quantise_x(1, 1)
         quantise_x(1, 2)
-        transpose_x(2)
-        for k in range(ORDERS):
-            quantise_x(2, k)
 
-        for h in range(HALVES):
-            passes(h, 0)
-            sums(h, 0, 0)
-            if h > 0:
-                sums(h - 1, 0, 1)
-            if h + 3 < HALVES:
-                transpose_x(h + 3)
+        done = []
+
+        def bank(h, r):
+            passes(h, r)
+            sums(h, r, 0)
+            if done:
+                sums(done[-1][0], done[-1][1], 1)
+            done.append((h, r))
+
+        for h in range(HALVES + LAG):
+            if h < HALVES:
+                bank(h, 0)
+            if h >= LAG:
+                bank(h - LAG, 1)
+            if h + 2 < HALVES:
+                transpose_x(h + 2)
                 for k in range(ORDERS):
-                    quantise_x(h + 3, k)
+                    quantise_x(h + 2, k)
+            if h == 0:
+                for k in range(ORDERS):
+                    regroup_w(1, k, False)
+            if h == 1:
+                for k in range(ORDERS):
+                    quantise_w(1, k)
             if h == 3:
                 emb_transposed()
-                regroup_w(1, 0, False)
-            if h == 4:
-                regroup_w(1, 1, False)
-                regroup_w(1, 2, True)
-                quantise_w(1, 0)
             if h == 5:
-                quantise_w(1, 1)
-                quantise_w(1, 2)
                 bias_term(0)
+                for k in range(ORDERS):
+                    regroup_w(2, k, False)
+            if h == 7:
+                for k in range(ORDERS):
+                    quantise_w(2, k)
         bias_term(1)
+        for k in range(ORDERS):
+            regroup_w(3, k, False)
         for r in range(2, ROUNDS):
-            for k in range(ORDERS):
-                regroup_w(r, k, False)
-        for r in range(1, ROUNDS):
             for h in range(HALVES):
-                passes(h, r)
-                sums(h, r, 0)
-                if h > 0:
-                    sums(h - 1, r, 1)
-                    if r == ROUNDS - 1:
-                        store(h - 1)
-                else:
-                    sums(HALVES - 1, r - 1, 1)
-                if r + 1 < ROUNDS and 4 <= h < 4 + ORDERS:
-                    quantise_w(r + 1, h - 4)
+                bank(h, r)
+                if r == ROUNDS - 1 and h > 0:
+                    store(h - 1)
+                if r + 1 < ROUNDS and 2 <= h < 2 + ORDERS:
+                    quantise_w(r + 1, h - 2)
         sums(HALVES - 1, ROUNDS - 1, 1)
         store(HALVES - 1)

@@ -194,6 +194,27 @@ def tile_dygcn_pb_kernel(tc, x_g, emb, weights_pool, bias_pool, out):
                             op1=ADD,
                         )
 
+        products = {}
+
+        def scale_bank(h, r):
+            z = banks[(h, r)]
+            prod = stage.tile([P, ROUND_SETS, PAIR, OUT], F32, name="products")
+            products[(h, r)] = prod
+            for i in range(PAIR):
+                for s in range(ROUND_SETS):
+                    col = (h * PAIR + i) * SETS + r * ROUND_SETS + s
+                    nc.scalar.activation(
+                        out=prod[:, s, i, :],
+                        in_=z[:, i, s * OUT : (s + 1) * OUT],
+                        func=mybir.ActivationFunctionType.Copy,
+                        scale=emb_f32[:, col : col + 1],
+                    )
+
+        def add_bank(h, r):
+            sums_now = acc[:, :, h * PAIR : (h + 1) * PAIR, :]
+            for s in range(0, ROUND_SETS, SLOTS):
+                nc.vector.tensor_add(out=sums_now, in0=sums_now, in1=products[(h, r)][:, s : s + SLOTS, :, :])
+
         def store(h):
             b, pr = divmod(h, TILES // PAIR)
             rows = slice(h * PAIR, (h + 1) * PAIR)
@@ -237,11 +258,23 @@ def tile_dygcn_pb_kernel(tc, x_g, emb, weights_pool, bias_pool, out):
 
         done = []
 
+        def by_scalar(h, r):
+            return r >= 2 and h % 2 == 0 and h < HALVES - 1
+
+        def finish(h, r):
+            if by_scalar(h, r):
+                add_bank(h, r)
+            else:
+                sums(h, r, 1)
+
         def bank(h, r):
             passes(h, r)
-            sums(h, r, 0)
+            if by_scalar(h, r):
+                scale_bank(h, r)
+            else:
+                sums(h, r, 0)
             if done:
-                sums(done[-1][0], done[-1][1], 1)
+                finish(done[-1][0], done[-1][1])
             done.append((h, r))
 
         for h in range(HALVES + LAG):

@@ -24,6 +24,8 @@ ROUND_SETS = 4
 ROUNDS = SETS // ROUND_SETS
 ROUND_COLS = ROUND_SETS * OUT
 SLOTS = 2
+DIAG = P // SETS
+GROUPS = ROWS // DIAG
 LAG = 3
 
 FLOPS = 2 * BATCH * NODES * ORDERS * FEAT * SETS * OUT
@@ -35,7 +37,7 @@ def tile_dygcn_pb_kernel(tc, x_g, emb, weights_pool, bias_pool, out):
         keep = ctx.enter_context(tc.tile_pool(name="keep", bufs=1))
         stage = ctx.enter_context(tc.tile_pool(name="stage", bufs=6))
         psum = ctx.enter_context(tc.psum_pool(name="psum", bufs=8))
-        ctx.enter_context(tc.manual_schedule(engines={mybir.EngineType.PE, mybir.EngineType.Activation}))
+        ctx.enter_context(tc.manual_schedule())
 
         x_raw = [
             [keep.tile([P, PAIR * FEAT], BF16, name="x_raw%d_%d" % (h, k)) for k in range(ORDERS)]
@@ -50,6 +52,12 @@ def tile_dygcn_pb_kernel(tc, x_g, emb, weights_pool, bias_pool, out):
         w_codes = [keep.tile([P, ORDERS, ROUND_COLS], U32, align_bytes=64, name="w_codes%d" % r) for r in range(ROUNDS)]
         w_scales = [keep.tile([P, ORDERS, ROUND_COLS], U8, align_bytes=64, name="w_scales%d" % r) for r in range(ROUNDS)]
         acc = keep.tile([P, SLOTS, ROWS, OUT], F32)
+
+        emb_bf = keep.tile([P, BATCH, TILES * SETS], BF16)
+        nc.scalar.dma_start(out=emb_bf[:], in_=emb.rearrange("b (p t) e -> p b (t e)", t=TILES))
+        bias_rows = keep.tile([P, OUT], BF16)
+        nc.vector.memset(bias_rows[:], 0.0)
+        nc.scalar.dma_start(out=bias_rows[0:SETS, :], in_=bias_pool)
 
         warm_in = keep.tile([P, 1], F32)
         warm_out = keep.tile([P, 1], F32)
@@ -78,39 +86,28 @@ def tile_dygcn_pb_kernel(tc, x_g, emb, weights_pool, bias_pool, out):
                     ),
                 )
 
-        emb_bf = keep.tile([P, BATCH, TILES * SETS], BF16)
-        nc.scalar.dma_start(out=emb_bf[:], in_=emb.rearrange("b (p t) e -> p b (t e)", t=TILES))
-        DIAG = P // SETS
-        GROUPS = ROWS // DIAG
-        bias_diag = keep.tile([P, DIAG * OUT], BF16)
-        nc.vector.memset(bias_diag[:], 0.0)
-
-        def load_bias(d):
-            nc.sync.dma_start(
-                out=bias_diag[d * SETS : (d + 1) * SETS, d * OUT : (d + 1) * OUT], in_=bias_pool
-            )
-
         load_x(0)
         load_w(0)
-        load_bias(0)
-        for h in range(1, 3):
-            load_x(h)
-            load_bias(h)
+        load_x(1)
+        load_x(2)
         load_w(1)
         for h in range(3, HALVES):
             load_x(h)
-            load_bias(h)
         load_w(2)
         load_w(3)
-
-
         w_grouped = [
             [keep.tile([P, ROUND_COLS, PACK], BF16, align_bytes=64, name="w_grouped%d_%d" % (r, k)) for k in range(ORDERS)]
             for r in range(ROUNDS)
         ]
 
         def regroup_w(r, k, on_vector):
-            if on_vector:
+            if on_vector is None:
+                nc.gpsimd.tensor_scalar(
+                    out=w_grouped[r][k][:].rearrange("p (e o) j -> p e o j", o=OUT),
+                    in0=w_raw[r][k][:].rearrange("p e (j o) -> p e o j", j=PACK),
+                    scalar1=1.0, scalar2=0.0, op0=MULT, op1=ADD,
+                )
+            elif on_vector:
                 nc.vector.tensor_copy(
                     out=w_grouped[r][k][:].rearrange("p (e c i) j -> p e c j i", e=ROUND_SETS, i=4),
                     in_=w_raw[r][k][:].rearrange("p e (j c i) -> p e c j i", j=PACK, i=4),
@@ -130,21 +127,31 @@ def tile_dygcn_pb_kernel(tc, x_g, emb, weights_pool, bias_pool, out):
 
         x_grouped = {}
 
-        def transpose_x(h):
-            for k in range(ORDERS):
-                words = x_raw[h][k][:].bitcast(F32)
-                xt = psum.tile([P, PAIR, 2, P], F32, name="bank")
-                for i in range(PAIR):
-                    for u in range(2):
-                        nc.tensor.transpose(
-                            xt[:, i, u, :], words[:, i * WORDS + u : (i + 1) * WORDS : 2], ident[:]
-                        )
-                grouped = stage.tile([P, PAIR * P * PACK], BF16, align_bytes=64, name="x_grouped")
-                x_grouped[(h, k)] = grouped
-                nc.scalar.copy(
-                    out=grouped[:].bitcast(F32).rearrange("p (i n u) -> p i n u", i=PAIR, u=2),
-                    in_=xt[:].rearrange("p i u n -> p i n u"),
-                )
+        x_sorted = {}
+
+        def sort_x(h, k, on_vector):
+            x_sorted[(h, k)] = stage.tile([P, PAIR, 2, P], F32, name="x_sorted")
+            copy = nc.vector.tensor_copy if on_vector else nc.scalar.copy
+            copy(
+                out=x_sorted[(h, k)][:],
+                in_=x_raw[h][k][:].bitcast(F32).rearrange("p (i w u) -> p i u w", i=PAIR, u=2),
+            )
+
+        def transpose_x(h, k):
+            xt = psum.tile([P, PAIR, 2, P], F32, name="bank")
+            for i in range(PAIR):
+                for u in range(2):
+                    if (h, k) in x_sorted:
+                        words = x_sorted[(h, k)][:, i, u, :]
+                    else:
+                        words = x_raw[h][k][:].bitcast(F32)[:, i * WORDS + u : (i + 1) * WORDS : 2]
+                    nc.tensor.transpose(xt[:, i, u, :], words, ident[:])
+            grouped = stage.tile([P, PAIR * P * PACK], BF16, align_bytes=64, name="x_grouped")
+            x_grouped[(h, k)] = grouped
+            nc.scalar.copy(
+                out=grouped[:].bitcast(F32).rearrange("p (i n u) -> p i n u", i=PAIR, u=2),
+                in_=xt[:].rearrange("p i u n -> p i n u"),
+            )
 
         def quantise_x(h, k):
             nc.vector.quantize_mx(
@@ -176,7 +183,16 @@ def tile_dygcn_pb_kernel(tc, x_g, emb, weights_pool, bias_pool, out):
                 for i in range(PAIR):
                     row = h * PAIR + i
                     col = row * SETS + r * ROUND_SETS + s
-                    if r == 0 and part == 0:
+                    if r == 0 and s == 0:
+                        nc.vector.scalar_tensor_tensor(
+                            out=acc[:, 0, row, :],
+                            in0=z[:, i, 0:OUT],
+                            scalar=emb_f32[:, col : col + 1],
+                            in1=bias_sum[:, row, :],
+                            op0=MULT,
+                            op1=ADD,
+                        )
+                    elif r == 0 and s == 1:
                         nc.vector.tensor_scalar(
                             out=acc[:, s, row, :],
                             in0=z[:, i, s * OUT : (s + 1) * OUT],
@@ -194,12 +210,11 @@ def tile_dygcn_pb_kernel(tc, x_g, emb, weights_pool, bias_pool, out):
                             op1=ADD,
                         )
 
-        products = {}
+        pairs = {}
 
         def scale_bank(h, r):
             z = banks[(h, r)]
             prod = stage.tile([P, ROUND_SETS, PAIR, OUT], F32, name="products")
-            products[(h, r)] = prod
             for i in range(PAIR):
                 for s in range(ROUND_SETS):
                     col = (h * PAIR + i) * SETS + r * ROUND_SETS + s
@@ -210,23 +225,48 @@ def tile_dygcn_pb_kernel(tc, x_g, emb, weights_pool, bias_pool, out):
                         scale=emb_f32[:, col : col + 1],
                     )
 
-        def add_bank(h, r):
-            sums_now = acc[:, :, h * PAIR : (h + 1) * PAIR, :]
-            for s in range(0, ROUND_SETS, SLOTS):
-                nc.vector.tensor_add(out=sums_now, in0=sums_now, in1=products[(h, r)][:, s : s + SLOTS, :, :])
+            pairs[(h, r)] = stage.tile([P, SLOTS, PAIR, OUT], F32, name="pairs")
+            nc.gpsimd.tensor_tensor(out=pairs[(h, r)][:], in0=prod[:, 0:SLOTS], in1=prod[:, SLOTS:], op=ADD)
 
-        def store(h):
+        def add_bank(h, r, engine):
+            sums_now = acc[:, :, h * PAIR : (h + 1) * PAIR, :]
+            engine.tensor_tensor(out=sums_now, in0=sums_now, in1=pairs[(h, r)][:], op=ADD)
+
+        def store(h, engine):
             b, pr = divmod(h, TILES // PAIR)
             rows = slice(h * PAIR, (h + 1) * PAIR)
-            result = stage.tile([P, PAIR, OUT], F32, name="result")
-            nc.vector.tensor_add(out=result[:], in0=acc[:, 0, rows, :], in1=acc[:, 1, rows, :])
+            result = keep.tile([P, PAIR, OUT], F32, name="result%d" % h)
+            engine.tensor_tensor(out=result[:], in0=acc[:, 0, rows, :], in1=acc[:, 1, rows, :], op=ADD)
             nc.sync.dma_start(
                 out=out[b].rearrange("(p t) o -> p (t o)", t=TILES)[:, pr * PAIR * OUT : (pr + 1) * PAIR * OUT],
                 in_=result[:].rearrange("p t o -> p (t o)"),
             )
 
         emb_f32 = keep.tile([P, ROWS * SETS], F32)
+        bias_sum = keep.tile([P, ROWS, OUT], F32)
+
         emb_t = keep.tile([P, GROUPS, P], BF16)
+        spread = keep.tile([P, DIAG, SETS], BF16)
+        block = keep.tile([P, DIAG], F32)
+        bias_diag = keep.tile([P, DIAG, OUT], BF16)
+
+        def bias_matrix():
+            nc.vector.tensor_copy(
+                out=spread[:], in_=ident[:, 0:SETS].rearrange("p (d e) -> p d e", d=1).to_broadcast([P, DIAG, SETS])
+            )
+            nc.vector.reduce_sum(
+                out=block[:], in_=ident[:].rearrange("p (d e) -> p d e", d=DIAG), axis=mybir.AxisListType.X
+            )
+            repeated = psum.tile([P, OUT], F32, name="bank")
+            nc.tensor.matmul(
+                repeated[:], lhsT=spread[:].rearrange("p d e -> p (d e)"), rhs=bias_rows[:], start=True, stop=True
+            )
+            nc.vector.tensor_tensor(
+                out=bias_diag[:],
+                in0=repeated[:].rearrange("p (d o) -> p d o", d=1).to_broadcast([P, DIAG, OUT]),
+                in1=block[:].rearrange("p (d o) -> p d o", o=1).to_broadcast([P, DIAG, OUT]),
+                op=MULT,
+            )
 
         def emb_transposed():
             emb_t_ps = psum.tile([P, GROUPS, P], F32, name="bank")
@@ -236,80 +276,144 @@ def tile_dygcn_pb_kernel(tc, x_g, emb, weights_pool, bias_pool, out):
 
         def bias_term(g):
             bias_ps = psum.tile([P, DIAG * OUT], F32, name="bank")
-            nc.tensor.matmul(bias_ps[:], lhsT=emb_t[:, g, :], rhs=bias_diag[:], start=True, stop=True)
-            rows = acc[:, 0, g * DIAG : (g + 1) * DIAG, :].rearrange("p d o -> p (d o)")
-            nc.vector.tensor_add(out=rows, in0=bias_ps[:], in1=rows)
+            nc.tensor.matmul(
+                bias_ps[:], lhsT=emb_t[:, g, :], rhs=bias_diag[:].rearrange("p d o -> p (d o)"), start=True, stop=True
+            )
+            nc.scalar.copy(
+                out=bias_sum[:, g * DIAG : (g + 1) * DIAG, :].rearrange("p d o -> p (d o)"), in_=bias_ps[:]
+            )
 
         nc.vector.tensor_copy(out=emb_f32[:], in_=emb_bf[:].rearrange("p b c -> p (b c)"))
-        transpose_x(0)
+        for k in range(ORDERS):
+            transpose_x(0, k)
+        bias_matrix()
+        emb_transposed()
         quantise_x(0, 0)
         regroup_w(0, 0, True)
         quantise_x(0, 1)
-        regroup_w(0, 1, True)
-        quantise_w(0, 0)
+        regroup_w(0, 1, False)
         quantise_x(0, 2)
+        quantise_w(0, 0)
         regroup_w(0, 2, True)
         quantise_w(0, 1)
-        transpose_x(1)
+        for k in range(ORDERS):
+            transpose_x(1, k)
+        for g in range(GROUPS):
+            bias_term(g)
         quantise_x(1, 0)
         quantise_w(0, 2)
         quantise_x(1, 1)
         quantise_x(1, 2)
 
+        last = {}
+
+        def last_passes(i):
+            h, r = HALVES - 1, ROUNDS - 1
+            last[i] = psum.tile([P, ROUND_COLS], F32, name="bank")
+            for k in range(ORDERS):
+                nc.tensor.matmul_mx(
+                    out=last[i][:],
+                    lhsT=x_codes[h][:, k, i * P : (i + 1) * P].bitcast(FP8X4),
+                    lhsT_scale=x_scales[h][:, k, i * P : (i + 1) * P],
+                    rhs=w_codes[r][:, k, :].bitcast(FP8X4),
+                    rhs_scale=w_scales[r][:, k, :],
+                    start=(k == 0),
+                    stop=(k == ORDERS - 1),
+                )
+
+        def last_sums(i, part):
+            row = ROWS - PAIR + i
+            for s in range(part * SLOTS, (part + 1) * SLOTS):
+                col = row * SETS + (ROUNDS - 1) * ROUND_SETS + s
+                nc.vector.scalar_tensor_tensor(
+                    out=acc[:, s % SLOTS, row, :],
+                    in0=last[i][:, s * OUT : (s + 1) * OUT],
+                    scalar=emb_f32[:, col : col + 1],
+                    in1=acc[:, s % SLOTS, row, :],
+                    op0=MULT,
+                    op1=ADD,
+                )
+
         done = []
 
         def by_scalar(h, r):
-            return r >= 2 and h % 2 == 0 and h < HALVES - 1
+            return h % 2 == 0 and r == ROUNDS - 2 or h in (1, 3) and r == ROUNDS - 1
 
-        def finish(h, r):
-            if by_scalar(h, r):
-                add_bank(h, r)
-            else:
-                sums(h, r, 1)
+        def finish(back):
+            if back < len(done):
+                h, r = done[-1 - back]
+                if back == 1 and not by_scalar(h, r):
+                    sums(h, r, 1)
+                if back == 3 and by_scalar(h, r) and r < ROUNDS - 1:
+                    add_bank(h, r, nc.vector)
 
         def bank(h, r):
             passes(h, r)
+            done.append((h, r))
             if by_scalar(h, r):
                 scale_bank(h, r)
+                if r == ROUNDS - 1:
+                    add_bank(h, r, nc.gpsimd)
+                    store(h, nc.gpsimd)
             else:
                 sums(h, r, 0)
-            if done:
-                finish(done[-1][0], done[-1][1])
-            done.append((h, r))
+            finish(1)
+            finish(3)
 
         for h in range(HALVES + LAG):
             if h < HALVES:
                 bank(h, 0)
+            if 0 < h < HALVES - 1:
+                for k in range(ORDERS):
+                    quantise_x(h + 1, k)
             if h >= LAG:
                 bank(h - LAG, 1)
             if h + 2 < HALVES:
-                transpose_x(h + 2)
                 for k in range(ORDERS):
-                    quantise_x(h + 2, k)
-            if h == 0:
-                for k in range(ORDERS):
-                    regroup_w(1, k, False)
+                    transpose_x(h + 2, k)
+                if h + 3 < HALVES and h + 3 >= 4:
+                    for k in range(2):
+                        sort_x(h + 3, k, k < 1)
+                if h == 0:
+                    regroup_w(1, 0, True)
+                if h == 1:
+                    regroup_w(1, 1, True)
+                if h == 1:
+                    regroup_w(1, 2, False)
             if h == 1:
-                for k in range(ORDERS):
-                    quantise_w(1, k)
-            if h == 3:
-                emb_transposed()
+                quantise_w(1, 0)
+            if h == 2:
+                quantise_w(1, 1)
+            if h == 2:
+                quantise_w(1, 2)
             if h == 5:
-                bias_term(0)
-                for k in range(ORDERS):
-                    regroup_w(2, k, False)
+                regroup_w(2, 0, False)
+            if h == 5:
+                regroup_w(2, 1, False)
+            if h == 5:
+                regroup_w(2, 2, False)
             if h == 7:
                 for k in range(ORDERS):
                     quantise_w(2, k)
-        bias_term(1)
         for k in range(ORDERS):
             regroup_w(3, k, False)
         for r in range(2, ROUNDS):
             for h in range(HALVES):
+                if (h, r) == (HALVES - 1, ROUNDS - 1):
+                    break
                 bank(h, r)
-                if r == ROUNDS - 1 and h > 0:
-                    store(h - 1)
+                if r == ROUNDS - 1 and h >= 2 and not by_scalar(h - 2, r):
+                    store(h - 2, nc.vector)
                 if r + 1 < ROUNDS and 2 <= h < 2 + ORDERS:
                     quantise_w(r + 1, h - 2)
-        sums(HALVES - 1, ROUNDS - 1, 1)
-        store(HALVES - 1)
+        h, r = HALVES - 1, ROUNDS - 1
+        for i in range(PAIR):
+            last_passes(i)
+        sums(h - 1, r, 1)
+        last_sums(0, 0)
+        store(h - 2, nc.vector)
+        last_sums(0, 1)
+        last_sums(1, 0)
+        store(h - 1, nc.vector)
+        last_sums(1, 1)
+        store(h, nc.vector)

@@ -337,7 +337,7 @@ def tile_dygcn_pb_kernel(tc, x_g, emb, weights_pool, bias_pool, out):
         done = []
 
         def by_scalar(h, r):
-            return h % 2 == 0 and r == ROUNDS - 2 or h in (1, 3) and r == ROUNDS - 1
+            return h % 2 == 0 and r == ROUNDS - 2 or h in (1, 4) and r == ROUNDS - 1
 
         def finish(back):
             if back < len(done):
@@ -355,25 +355,30 @@ def tile_dygcn_pb_kernel(tc, x_g, emb, weights_pool, bias_pool, out):
                 if r == ROUNDS - 1:
                     add_bank(h, r, nc.gpsimd)
                     store(h, nc.gpsimd)
-            else:
+            if r == ROUNDS - 1:
+                finish(1)
+            if not by_scalar(h, r):
                 sums(h, r, 0)
-            finish(1)
+            if r < ROUNDS - 1:
+                finish(1)
             finish(3)
 
         for h in range(HALVES + LAG):
+            if h == HALVES - 1:
+                bank(h - LAG, 1)
             if h < HALVES:
                 bank(h, 0)
             if 0 < h < HALVES - 1:
                 for k in range(ORDERS):
                     quantise_x(h + 1, k)
-            if h >= LAG:
+            if h >= LAG and h != HALVES - 1:
                 bank(h - LAG, 1)
             if h + 2 < HALVES:
                 for k in range(ORDERS):
                     transpose_x(h + 2, k)
-                if h + 3 < HALVES and h + 3 >= 4:
-                    for k in range(2):
-                        sort_x(h + 3, k, k < 1)
+                if 5 <= h + 3 < HALVES:
+                    for k in range(ORDERS):
+                        sort_x(h + 3, k, k == 0)
                 if h == 0:
                     regroup_w(1, 0, True)
                 if h == 1:

from contextlib import ExitStack

import concourse.mybir as mybir
from concourse.masks import make_identity

BF16 = mybir.dt.bfloat16
F32 = mybir.dt.float32
U32 = mybir.dt.uint32
U8 = mybir.dt.uint8
FP8X4 = mybir.dt.float8_e4m3fn_x4
MULT = mybir.AluOpType.mult
ADD = mybir.AluOpType.add

P = 128
PACK = 4
BATCH, ORDERS, NODES, FEAT = 4, 3, 512, 512
SETS, OUT = 16, 64
TILES = NODES // P
ROWS = BATCH * TILES
PAIR = 2
HALVES = ROWS // PAIR
WORDS = FEAT // 2
ROUND_SETS = 4
ROUNDS = SETS // ROUND_SETS
ROUND_COLS = ROUND_SETS * OUT
SLOTS = 2
DIAG = P // SETS
GROUPS = ROWS // DIAG
LAG = 3

FLOPS = 2 * BATCH * NODES * ORDERS * FEAT * SETS * OUT


def tile_dygcn_pb_kernel(tc, x_g, emb, weights_pool, bias_pool, out):
    nc = tc.nc
    with ExitStack() as ctx:
        keep = ctx.enter_context(tc.tile_pool(name="keep", bufs=1))
        stage = ctx.enter_context(tc.tile_pool(name="stage", bufs=6))
        psum = ctx.enter_context(tc.psum_pool(name="psum", bufs=8))
        ctx.enter_context(tc.manual_schedule())

        x_raw = [
            [keep.tile([P, PAIR * FEAT], BF16, name="x_raw%d_%d" % (h, k)) for k in range(ORDERS)]
            for h in range(HALVES)
        ]
        w_raw = [
            [keep.tile([P, ROUND_SETS, PACK * OUT], BF16, name="w_raw%d_%d" % (r, k)) for k in range(ORDERS)]
            for r in range(ROUNDS)
        ]
        x_codes = [keep.tile([P, ORDERS, PAIR * P], U32, align_bytes=64, name="x_codes%d" % h) for h in range(HALVES)]
        x_scales = [keep.tile([P, ORDERS, PAIR * P], U8, align_bytes=64, name="x_scales%d" % h) for h in range(HALVES)]
        w_codes = [keep.tile([P, ORDERS, ROUND_COLS], U32, align_bytes=64, name="w_codes%d" % r) for r in range(ROUNDS)]
        w_scales = [keep.tile([P, ORDERS, ROUND_COLS], U8, align_bytes=64, name="w_scales%d" % r) for r in range(ROUNDS)]
        acc = keep.tile([P, SLOTS, ROWS, OUT], F32)

        emb_bf = keep.tile([P, BATCH, TILES * SETS], BF16)
        nc.scalar.dma_start(out=emb_bf[:], in_=emb.rearrange("b (p t) e -> p b (t e)", t=TILES))
        bias_rows = keep.tile([P, OUT], BF16)
        nc.vector.memset(bias_rows[:], 0.0)
        nc.scalar.dma_start(out=bias_rows[0:SETS, :], in_=bias_pool)

        warm_in = keep.tile([P, 1], F32)
        warm_out = keep.tile([P, 1], F32)
        nc.vector.memset(warm_in[:], 0.0)
        nc.scalar.copy(out=warm_out[:], in_=warm_in[:])

        ident = keep.tile([P, P], F32)
        make_identity(nc, ident[:])

        def load_x(h):
            b, pr = divmod(h, TILES // PAIR)
            for k in range(ORDERS):
                nc.sync.dma_start(
                    out=x_raw[h][k][:],
                    in_=x_g[b, k].rearrange("(p t) f -> p (t f)", t=TILES)[
                        :, pr * PAIR * FEAT : (pr + 1) * PAIR * FEAT
                    ],
                )

        def load_w(r):
            for k in range(ORDERS):
                nc.sync.dma_start(
                    out=w_raw[r][k][:],
                    in_=weights_pool[r * ROUND_SETS : (r + 1) * ROUND_SETS, k, :, :].rearrange(
                        "e (p j) o -> p e (j o)", j=PACK
                    ),
                )

        load_x(0)
        load_w(0)
        load_x(1)
        load_x(2)
        load_w(1)
        for h in range(3, HALVES):
            load_x(h)
        load_w(2)
        load_w(3)
        w_grouped = [
            [keep.tile([P, ROUND_COLS, PACK], BF16, align_bytes=64, name="w_grouped%d_%d" % (r, k)) for k in range(ORDERS)]
            for r in range(ROUNDS)
        ]

        def regroup_w(r, k, on_vector):
            if on_vector is None:
                nc.gpsimd.tensor_scalar(
                    out=w_grouped[r][k][:].rearrange("p (e o) j -> p e o j", o=OUT),
                    in0=w_raw[r][k][:].rearrange("p e (j o) -> p e o j", j=PACK),
                    scalar1=1.0, scalar2=0.0, op0=MULT, op1=ADD,
                )
            elif on_vector:
                nc.vector.tensor_copy(
                    out=w_grouped[r][k][:].rearrange("p (e c i) j -> p e c j i", e=ROUND_SETS, i=4),
                    in_=w_raw[r][k][:].rearrange("p e (j c i) -> p e c j i", j=PACK, i=4),
                )
            else:
                nc.scalar.copy(
                    out=w_grouped[r][k][:].rearrange("p (e o) j -> p e o j", o=OUT),
                    in_=w_raw[r][k][:].rearrange("p e (j o) -> p e o j", j=PACK),
                )

        def quantise_w(r, k):
            nc.vector.quantize_mx(
                out=w_codes[r][:, k, :].bitcast(FP8X4),
                scales=w_scales[r][:, k, :],
                in_=w_grouped[r][k][:].rearrange("p c j -> p (c j)"),
            )

        x_grouped = {}

        x_sorted = {}

        def sort_x(h, k, on_vector):
            x_sorted[(h, k)] = stage.tile([P, PAIR, 2, P], F32, name="x_sorted")
            copy = nc.vector.tensor_copy if on_vector else nc.scalar.copy
            copy(
                out=x_sorted[(h, k)][:],
                in_=x_raw[h][k][:].bitcast(F32).rearrange("p (i w u) -> p i u w", i=PAIR, u=2),
            )

        def transpose_x(h, k):
            xt = psum.tile([P, PAIR, 2, P], F32, name="bank")
            for i in range(PAIR):
                for u in range(2):
                    if (h, k) in x_sorted:
                        words = x_sorted[(h, k)][:, i, u, :]
                    else:
                        words = x_raw[h][k][:].bitcast(F32)[:, i * WORDS + u : (i + 1) * WORDS : 2]
                    nc.tensor.transpose(xt[:, i, u, :], words, ident[:])
            grouped = stage.tile([P, PAIR * P * PACK], BF16, align_bytes=64, name="x_grouped")
            x_grouped[(h, k)] = grouped
            nc.scalar.copy(
                out=grouped[:].bitcast(F32).rearrange("p (i n u) -> p i n u", i=PAIR, u=2),
                in_=xt[:].rearrange("p i u n -> p i n u"),
            )

        def quantise_x(h, k):
            nc.vector.quantize_mx(
                out=x_codes[h][:, k, :].bitcast(FP8X4),
                scales=x_scales[h][:, k, :],
                in_=x_grouped[(h, k)][:],
            )

        banks = {}

        def passes(h, r):
            z = psum.tile([P, PAIR, ROUND_COLS], F32, name="bank")
            banks[(h, r)] = z
            for i in range(PAIR):
                for k in range(ORDERS):
                    nc.tensor.matmul_mx(
                        out=z[:, i, :],
                        lhsT=x_codes[h][:, k, i * P : (i + 1) * P].bitcast(FP8X4),
                        lhsT_scale=x_scales[h][:, k, i * P : (i + 1) * P],
                        rhs=w_codes[r][:, k, :].bitcast(FP8X4),
                        rhs_scale=w_scales[r][:, k, :],
                        start=(k == 0),
                        stop=(k == ORDERS - 1),
                    )

        def sums(h, r, part):
            z = banks[(h, r)]
            for s in range(part * SLOTS, (part + 1) * SLOTS):
                for i in range(PAIR):
                    row = h * PAIR + i
                    col = row * SETS + r * ROUND_SETS + s
                    if r == 0 and s == 0:
                        nc.vector.scalar_tensor_tensor(
                            out=acc[:, 0, row, :],
                            in0=z[:, i, 0:OUT],
                            scalar=emb_f32[:, col : col + 1],
                            in1=bias_sum[:, row, :],
                            op0=MULT,
                            op1=ADD,
                        )
                    elif r == 0 and s == 1:
                        nc.vector.tensor_scalar(
                            out=acc[:, s, row, :],
                            in0=z[:, i, s * OUT : (s + 1) * OUT],
                            scalar1=emb_f32[:, col : col + 1],
                            scalar2=None,
                            op0=MULT,
                        )
                    else:
                        nc.vector.scalar_tensor_tensor(
                            out=acc[:, s % SLOTS, row, :],
                            in0=z[:, i, s * OUT : (s + 1) * OUT],
                            scalar=emb_f32[:, col : col + 1],
                            in1=acc[:, s % SLOTS, row, :],
                            op0=MULT,
                            op1=ADD,
                        )

        pairs = {}

        def scale_bank(h, r):
            z = banks[(h, r)]
            prod = stage.tile([P, ROUND_SETS, PAIR, OUT], F32, name="products")
            for i in range(PAIR):
                for s in range(ROUND_SETS):
                    col = (h * PAIR + i) * SETS + r * ROUND_SETS + s
                    nc.scalar.activation(
                        out=prod[:, s, i, :],
                        in_=z[:, i, s * OUT : (s + 1) * OUT],
                        func=mybir.ActivationFunctionType.Copy,
                        scale=emb_f32[:, col : col + 1],
                    )

            pairs[(h, r)] = stage.tile([P, SLOTS, PAIR, OUT], F32, name="pairs")
            nc.gpsimd.tensor_tensor(out=pairs[(h, r)][:], in0=prod[:, 0:SLOTS], in1=prod[:, SLOTS:], op=ADD)

        def add_bank(h, r, engine):
            sums_now = acc[:, :, h * PAIR : (h + 1) * PAIR, :]
            engine.tensor_tensor(out=sums_now, in0=sums_now, in1=pairs[(h, r)][:], op=ADD)

        def store(h, engine):
            b, pr = divmod(h, TILES // PAIR)
            rows = slice(h * PAIR, (h + 1) * PAIR)
            result = keep.tile([P, PAIR, OUT], F32, name="result%d" % h)
            engine.tensor_tensor(out=result[:], in0=acc[:, 0, rows, :], in1=acc[:, 1, rows, :], op=ADD)
            nc.sync.dma_start(
                out=out[b].rearrange("(p t) o -> p (t o)", t=TILES)[:, pr * PAIR * OUT : (pr + 1) * PAIR * OUT],
                in_=result[:].rearrange("p t o -> p (t o)"),
            )

        emb_f32 = keep.tile([P, ROWS * SETS], F32)
        bias_sum = keep.tile([P, ROWS, OUT], F32)

        emb_t = keep.tile([P, GROUPS, P], BF16)
        spread = keep.tile([P, DIAG, SETS], BF16)
        block = keep.tile([P, DIAG], F32)
        bias_diag = keep.tile([P, DIAG, OUT], BF16)

        def bias_matrix():
            nc.vector.tensor_copy(
                out=spread[:], in_=ident[:, 0:SETS].rearrange("p (d e) -> p d e", d=1).to_broadcast([P, DIAG, SETS])
            )
            nc.vector.reduce_sum(
                out=block[:], in_=ident[:].rearrange("p (d e) -> p d e", d=DIAG), axis=mybir.AxisListType.X
            )
            repeated = psum.tile([P, OUT], F32, name="bank")
            nc.tensor.matmul(
                repeated[:], lhsT=spread[:].rearrange("p d e -> p (d e)"), rhs=bias_rows[:], start=True, stop=True
            )
            nc.vector.tensor_tensor(
                out=bias_diag[:],
                in0=repeated[:].rearrange("p (d o) -> p d o", d=1).to_broadcast([P, DIAG, OUT]),
                in1=block[:].rearrange("p (d o) -> p d o", o=1).to_broadcast([P, DIAG, OUT]),
                op=MULT,
            )

        def emb_transposed():
            emb_t_ps = psum.tile([P, GROUPS, P], F32, name="bank")
            for g in range(GROUPS):
                nc.tensor.transpose(emb_t_ps[:, g, :], emb_f32[:, g * P : (g + 1) * P], ident[:])
            nc.scalar.copy(out=emb_t[:], in_=emb_t_ps[:])

        def bias_term(g):
            bias_ps = psum.tile([P, DIAG * OUT], F32, name="bank")
            nc.tensor.matmul(
                bias_ps[:], lhsT=emb_t[:, g, :], rhs=bias_diag[:].rearrange("p d o -> p (d o)"), start=True, stop=True
            )
            nc.scalar.copy(
                out=bias_sum[:, g * DIAG : (g + 1) * DIAG, :].rearrange("p d o -> p (d o)"), in_=bias_ps[:]
            )

        nc.vector.tensor_copy(out=emb_f32[:], in_=emb_bf[:].rearrange("p b c -> p (b c)"))
        for k in range(ORDERS):
            transpose_x(0, k)
        bias_matrix()
        emb_transposed()
        quantise_x(0, 0)
        regroup_w(0, 0, True)
        quantise_x(0, 1)
        regroup_w(0, 1, False)
        quantise_x(0, 2)
        quantise_w(0, 0)
        regroup_w(0, 2, True)
        quantise_w(0, 1)
        for k in range(ORDERS):
            transpose_x(1, k)
        for g in range(GROUPS):
            bias_term(g)
        quantise_x(1, 0)
        quantise_w(0, 2)
        quantise_x(1, 1)
        quantise_x(1, 2)

        last = {}

        def last_passes(i):
            h, r = HALVES - 1, ROUNDS - 1
            last[i] = psum.tile([P, ROUND_COLS], F32, name="bank")
            for k in range(ORDERS):
                nc.tensor.matmul_mx(
                    out=last[i][:],
                    lhsT=x_codes[h][:, k, i * P : (i + 1) * P].bitcast(FP8X4),
                    lhsT_scale=x_scales[h][:, k, i * P : (i + 1) * P],
                    rhs=w_codes[r][:, k, :].bitcast(FP8X4),
                    rhs_scale=w_scales[r][:, k, :],
                    start=(k == 0),
                    stop=(k == ORDERS - 1),
                )

        def last_sums(i, part):
            row = ROWS - PAIR + i
            for s in range(part * SLOTS, (part + 1) * SLOTS):
                col = row * SETS + (ROUNDS - 1) * ROUND_SETS + s
                nc.vector.scalar_tensor_tensor(
                    out=acc[:, s % SLOTS, row, :],
                    in0=last[i][:, s * OUT : (s + 1) * OUT],
                    scalar=emb_f32[:, col : col + 1],
                    in1=acc[:, s % SLOTS, row, :],
                    op0=MULT,
                    op1=ADD,
                )

        done = []

        def by_scalar(h, r):
            return h % 2 == 0 and r == ROUNDS - 2 or h in (1, 4) and r == ROUNDS - 1

        def finish(back):
            if back < len(done):
                h, r = done[-1 - back]
                if back == 1 and not by_scalar(h, r):
                    sums(h, r, 1)
                if back == 3 and by_scalar(h, r) and r < ROUNDS - 1:
                    add_bank(h, r, nc.vector)

        def bank(h, r):
            passes(h, r)
            done.append((h, r))
            if by_scalar(h, r):
                scale_bank(h, r)
                if r == ROUNDS - 1:
                    add_bank(h, r, nc.gpsimd)
                    store(h, nc.gpsimd)
            if r == ROUNDS - 1:
                finish(1)
            if not by_scalar(h, r):
                sums(h, r, 0)
            if r < ROUNDS - 1:
                finish(1)
            finish(3)

        for h in range(HALVES + LAG):
            if h == HALVES - 1:
                bank(h - LAG, 1)
            if h < HALVES:
                bank(h, 0)
            if 0 < h < HALVES - 1:
                for k in range(ORDERS):
                    quantise_x(h + 1, k)
            if h >= LAG and h != HALVES - 1:
                bank(h - LAG, 1)
            if h + 2 < HALVES:
                for k in range(ORDERS):
                    transpose_x(h + 2, k)
                if 5 <= h + 3 < HALVES:
                    for k in range(ORDERS):
                        sort_x(h + 3, k, k == 0)
                if h == 0:
                    regroup_w(1, 0, True)
                if h == 1:
                    regroup_w(1, 1, True)
                if h == 1:
                    regroup_w(1, 2, False)
            if h == 1:
                quantise_w(1, 0)
            if h == 2:
                quantise_w(1, 1)
            if h == 2:
                quantise_w(1, 2)
            if h == 5:
                regroup_w(2, 0, False)
            if h == 5:
                regroup_w(2, 1, False)
            if h == 5:
                regroup_w(2, 2, False)
            if h == 7:
                for k in range(ORDERS):
                    quantise_w(2, k)
        for k in range(ORDERS):
            regroup_w(3, k, False)
        for r in range(2, ROUNDS):
            for h in range(HALVES):
                if (h, r) == (HALVES - 1, ROUNDS - 1):
                    break
                bank(h, r)
                if r == ROUNDS - 1 and h >= 2 and not by_scalar(h - 2, r):
                    store(h - 2, nc.vector)
                if r + 1 < ROUNDS and 2 <= h < 2 + ORDERS:
                    quantise_w(r + 1, h - 2)
        h, r = HALVES - 1, ROUNDS - 1
        for i in range(PAIR):
            last_passes(i)
        sums(h - 1, r, 1)
        last_sums(0, 0)
        store(h - 2, nc.vector)
        last_sums(0, 1)
        last_sums(1, 0)
        store(h - 1, nc.vector)
        last_sums(1, 1)
        store(h, nc.vector)
